import numpy as np
import ml_dtypes


def mxq(x, axis, fmt="e4m3"):
    dtype, down = {"e4m3": (ml_dtypes.float8_e4m3fn, 7), "e5m2": (ml_dtypes.float8_e5m2, 14)}[fmt]
    v = np.moveaxis(np.asarray(x, np.float32).astype(ml_dtypes.bfloat16).astype(np.float64), axis, -1)
    blocks = v.reshape(v.shape[:-1] + (-1, 32))
    amax = np.abs(blocks).max(-1, keepdims=True)
    byte = np.maximum(np.where(amax > 0, np.frexp(amax)[1] - 1 + 127, 0) - down, 1)
    scale = np.exp2(byte - 127.0)
    codes = (blocks / scale).astype(np.float32).astype(dtype).astype(np.float64)
    return np.moveaxis((codes * scale).reshape(v.shape), -1, axis)


WIDE = False


def mx_kscale(k):
    if not WIDE:
        return np.ones(k)
    levels = np.array([10, -10, 5, -5, 0])
    if k % 512:
        return np.exp2(np.random.permutation(np.resize(levels, k // 32))).repeat(32)
    a = np.empty((k // 512, 16))
    for p in range(k // 512):
        a[p, :8] = np.random.permutation(np.resize(levels, 8))
        for g in range(8):
            far = levels[np.abs(levels - a[p, g]) >= 10]
            a[p, g + 8] = far[np.random.randint(len(far))]
    return np.exp2(a.ravel()).repeat(32)


BF16 = ml_dtypes.bfloat16


def bf(x):
    return np.asarray(x, np.float32).astype(BF16)


def f64(x):
    return np.asarray(x).astype(np.float64)


B, N, E, H, C = 4, 1024, 1024, 4, 512
D = E // H
EPS = 1e-5


def silu(t):
    return t / (1.0 + np.exp(-t))


def setup_inputs():
    t = mx_kscale(E)
    ret = np.random.standard_normal((B, N, H, D)) * 4.0 + np.random.standard_normal((B, N, H, 1)) * 2.0
    return {"ret": bf(ret.reshape(B, N, E)),
            "g": bf(np.random.standard_normal((B, N, E))),
            "gn_weight": bf((1.0 + 0.1 * np.random.standard_normal(E)) * t),
            "gn_bias": bf(0.1 * np.random.standard_normal(E) * t),
            "w_o": bf(np.random.standard_normal((E, E)) / np.sqrt(E) / t[:, None]),
            "b_o": bf(np.random.standard_normal(E) * 0.3)}


def reference(ret, g, gn_weight, gn_bias, w_o, b_o):
    r = f64(ret).reshape(B, N, H, D)
    mean = r.mean(axis=-1, keepdims=True)
    var = r.var(axis=-1, keepdims=True)
    r = (r - mean) / np.sqrt(var + EPS)
    rn = r.reshape(B, N, E) * f64(gn_weight) + f64(gn_bias)
    gate = silu(f64(g)) * rn
    return (mxq(gate, 2, "e4m3") @ mxq(f64(w_o), 0, "e4m3")) + f64(b_o)

@@ -1,0 +1,274 @@
+from contextlib import ExitStack
+
+import concourse.mybir as mybir
+from concourse.masks import make_identity
+
+F32 = mybir.dt.float32
+BF16 = mybir.dt.bfloat16
+U32 = mybir.dt.uint32
+U8 = mybir.dt.uint8
+FP8X4 = mybir.dt.float8_e4m3fn_x4
+ALU = mybir.AluOpType
+ACT = mybir.ActivationFunctionType
+
+P = 128
+PACK = 4
+K_PASS = P * PACK
+TOKENS = 4 * 1024
+E = 1024
+HEADS = 4
+HEAD = E // HEADS
+EPS = 1e-5
+PASSES = E // K_PASS
+K_BLOCKS = E // P
+TILES = 2
+TOK = TILES * P
+ROUNDS = TOKENS // TOK
+GROUPS = TILES * HEADS
+N_BANK = 512
+N_HALVES = E // N_BANK
+RUN = 4
+PAIR = 2
+AHEAD = 3
+
+FLOPS = 2 * TOKENS * E * E
+
+
+def tile_multiscaleretention_pc_t_kernel(tc, ret, g, gn_weight, gn_bias, w_o, b_o, out):
+    nc = tc.nc
+    ret_rounds = ret.flatten_outer_dims().rearrange("(r p j) c -> r p j c", p=P, j=TILES)
+    g_rounds = g.flatten_outer_dims().rearrange("(r p j) c -> r p j c", p=P, j=TILES)
+    out_rounds = out.flatten_outer_dims().rearrange("(r p j) c -> r p j c", p=P, j=TILES)
+    w_passes = w_o.rearrange("(c p t) n -> c p t n", t=PACK, p=P)
+
+    with ExitStack() as ctx:
+        const = ctx.enter_context(tc.tile_pool(name="const", bufs=1))
+        w_stage = ctx.enter_context(tc.tile_pool(name="w_stage", bufs=2))
+        x_pool = ctx.enter_context(tc.tile_pool(name="x", bufs=AHEAD + 3))
+        g_pool = ctx.enter_context(tc.tile_pool(name="g", bufs=4))
+        small = ctx.enter_context(tc.tile_pool(name="small", bufs=AHEAD + 2))
+        r_pool = ctx.enter_context(tc.tile_pool(name="r", bufs=3))
+        t_pool = ctx.enter_context(tc.tile_pool(name="transposed", bufs=4))
+        q_pool = ctx.enter_context(tc.tile_pool(name="quantised", bufs=3))
+        o_pool = ctx.enter_context(tc.tile_pool(name="o", bufs=3))
+        psum_r = ctx.enter_context(tc.psum_pool(name="psum_r", bufs=4))
+        psum_g = ctx.enter_context(tc.psum_pool(name="psum_g", bufs=2))
+        psum_o = ctx.enter_context(tc.psum_pool(name="psum_o", bufs=2))
+        ctx.enter_context(tc.manual_schedule())
+
+        x_of, g_of, stats_of, rstd_of, shift_of, r_of, gate_of, codes_of, scales_of, out_of = (
+            {}, {}, {}, {}, {}, {}, {}, {}, {}, {},
+        )
+        g_bank_of, r_banks_of, silu_of, rn_of, acc_of = {}, {}, {}, {}, {}
+        w_raw_of, w_grouped_of = {}, {}
+
+        def load_ret(r):
+            x_of[r] = x_pool.tile([P, TILES, E], BF16, name="x_sb")
+            nc.sync.dma_start(out=x_of[r][:], in_=ret_rounds[r])
+
+        def load_g(r):
+            g_of[r] = g_pool.tile([P, TILES, E], BF16, name="g_sb")
+            nc.sync.dma_start(out=g_of[r][:], in_=g_rounds[r])
+
+        def statistics(r):
+            stats = small.tile([P, GROUPS, 3], F32, name="stats")
+            for j in range(TILES):
+                for pair in range(HEADS // 2):
+                    i = j * HEADS + 2 * pair
+                    nc.vector.bn_stats(
+                        out=stats[:, i : i + 2, :].rearrange("p a s -> p (a s)"),
+                        in_=x_of[r][:, j, 2 * pair * HEAD : 2 * (pair + 1) * HEAD].rearrange("p (a d) -> p d a", a=2),
+                    )
+            stats_of[r] = stats
+
+        def scale_and_shift(r):
+            mean, count_var = stats_of[r][:, :, 1], stats_of[r][:, :, 2]
+            var_eps = small.tile([P, GROUPS], F32, name="var_eps")
+            nc.gpsimd.tensor_scalar(
+                out=var_eps[:], in0=count_var, scalar1=1.0 / HEAD, scalar2=EPS, op0=ALU.mult, op1=ALU.add
+            )
+            minus_mean = small.tile([P, GROUPS], F32, name="minus_mean")
+            nc.gpsimd.tensor_scalar(out=minus_mean[:], in0=mean, scalar1=-1.0, scalar2=0.0, op0=ALU.mult, op1=ALU.add)
+            rstd_of[r] = small.tile([P, GROUPS], F32, name="rstd")
+            nc.gpsimd.tensor_tensor(out=rstd_of[r][:], in0=var_eps[:], in1=minus_half[:], op=ALU.pow)
+            shift_of[r] = small.tile([P, GROUPS], F32, name="shift")
+            nc.gpsimd.tensor_tensor(out=shift_of[r][:], in0=minus_mean[:], in1=rstd_of[r][:], op=ALU.mult)
+
+        def normalise(r):
+            r_of[r] = r_pool.tile([P, TILES, E], F32, name="r_sb")
+            for j in range(TILES):
+                for h in range(HEADS):
+                    i = j * HEADS + h
+                    cols = slice(h * HEAD, (h + 1) * HEAD)
+                    nc.scalar.activation(
+                        out=r_of[r][:, j, cols], in_=x_of[r][:, j, cols], func=ACT.Identity,
+                        scale=rstd_of[r][:, i : i + 1], bias=shift_of[r][:, i : i + 1],
+                    )
+
+        def transpose_g(r, c):
+            g_bank = psum_g.tile([P, PACK, TOK], BF16, name="g_bank")
+            for t in range(PACK):
+                for j in range(TILES):
+                    nc.tensor.transpose(
+                        g_bank[:, t, j * P : (j + 1) * P],
+                        g_of[r][:, j, c * K_PASS + t : (c + 1) * K_PASS : PACK],
+                        ident_bf16[:],
+                    )
+            g_bank_of[r, c] = g_bank
+
+        def transpose_r(r, c):
+            r_banks_of[r, c] = []
+            for half in range(PACK // 2):
+                r_bank = psum_r.tile([P, 2, TOK], F32, name="r_bank")
+                for i in range(2):
+                    t = 2 * half + i
+                    for j in range(TILES):
+                        nc.tensor.transpose(
+                            r_bank[:, i, j * P : (j + 1) * P],
+                            r_of[r][:, j, c * K_PASS + t : (c + 1) * K_PASS : PACK],
+                            ident_f32[:],
+                        )
+                r_banks_of[r, c].append(r_bank)
+
+        def leave_psum(r, c):
+            silu_of[r, c] = t_pool.tile([P, PACK, TOK], F32, name="silu_t")
+            nc.scalar.activation(out=silu_of[r, c][:], in_=g_bank_of[r, c][:], func=ACT.Silu)
+            rn_of[r, c] = t_pool.tile([P, PACK, TOK], F32, name="rn_t")
+            for t in range(PACK):
+                m = c * PACK + t
+                nc.scalar.activation(
+                    out=rn_of[r, c][:, t, :], in_=r_banks_of[r, c][t // 2][:, t % 2, :], func=ACT.Identity,
+                    scale=weight_col[:, m : m + 1], bias=bias_col[:, m : m + 1],
+                )
+
+        def product(r, c):
+            if c == 0:
+                gate_of[r] = q_pool.tile([P, PASSES, TOK, PACK], BF16, name="gate", align_bytes=64)
+            nc.vector.tensor_tensor(
+                out=gate_of[r][:, c].rearrange("p (q i) t -> p q t i", i=PAIR),
+                in0=rn_of[r, c][:].rearrange("p t (q i) -> p q t i", i=PAIR),
+                in1=silu_of[r, c][:].rearrange("p t (q i) -> p q t i", i=PAIR),
+                op=ALU.mult,
+            )
+
+        def quantise(r):
+            codes_of[r] = q_pool.tile([P, PASSES, TOK], U32, name="codes", align_bytes=64)
+            scales_of[r] = q_pool.tile([P, PASSES, TOK], U8, name="scales", align_bytes=64)
+            nc.vector.quantize_mx(
+                out=codes_of[r][:].rearrange("p c k -> p (c k)").bitcast(FP8X4),
+                scales=scales_of[r][:].rearrange("p c k -> p (c k)"),
+                in_=gate_of[r][:].rearrange("p c k t -> p (c k t)"),
+            )
+
+        def matmuls(r, j):
+            tokens = slice(j * P, (j + 1) * P)
+            for n in range(N_HALVES):
+                n_cols = slice(n * N_BANK, (n + 1) * N_BANK)
+                acc_of[r, j, n] = psum_o.tile([P, N_BANK], F32, name="acc")
+                for c in range(PASSES):
+                    nc.tensor.matmul_mx(
+                        out=acc_of[r, j, n][:],
+                        lhsT=codes_of[r][:, c, tokens].bitcast(FP8X4),
+                        lhsT_scale=scales_of[r][:, c, tokens],
+                        rhs=w_codes[:, c, n_cols].bitcast(FP8X4),
+                        rhs_scale=w_scales[:, c, n_cols],
+                        start=(c == 0),
+                        stop=(c == PASSES - 1),
+                    )
+
+        def add_bias(r, j):
+            if j == 0:
+                out_of[r] = o_pool.tile([P, TILES, E], F32, name="out_sb")
+            for n in range(N_HALVES):
+                n_cols = slice(n * N_BANK, (n + 1) * N_BANK)
+                nc.vector.tensor_tensor(
+                    out=out_of[r][:, j, n_cols], in0=acc_of[r, j, n][:], in1=b_all[:, n_cols], op=ALU.add
+                )
+
+        def store(r):
+            nc.sync.dma_start(out=out_rounds[r], in_=out_of[r][:])
+
+        def load_w(c):
+            w_raw_of[c] = w_stage.tile([P, PACK, E], BF16, name="w_raw")
+            nc.sync.dma_start(out=w_raw_of[c][:], in_=w_passes[c])
+
+        def regroup_w(c):
+            w_grouped_of[c] = w_stage.tile([P, E, PACK], BF16, name="w_grouped", align_bytes=64)
+            nc.vector.tensor_copy(
+                out=w_grouped_of[c][:].rearrange("p (q i) t -> p q t i", i=RUN),
+                in_=w_raw_of[c][:].rearrange("p t (q i) -> p q t i", i=RUN),
+            )
+
+        def quantise_w(c):
+            nc.vector.quantize_mx(
+                out=w_codes[:, c, :].bitcast(FP8X4),
+                scales=w_scales[:, c, :],
+                in_=w_grouped_of[c][:].rearrange("p n t -> p (n t)"),
+            )
+
+        ident_f32 = const.tile([P, P], F32, name="ident_f32")
+        make_identity(nc, ident_f32[:])
+        ident_bf16 = const.tile([P, P], BF16, name="ident_bf16")
+        make_identity(nc, ident_bf16[:])
+        minus_half = const.tile([P, GROUPS], F32, name="minus_half")
+        nc.gpsimd.memset(minus_half[:], -0.5)
+        w_codes = const.tile([P, PASSES, E], U32, name="w_codes", align_bytes=64)
+        w_scales = const.tile([P, PASSES, E], U8, name="w_scales", align_bytes=64)
+
+        weight_raw = const.tile([P, PASSES, PACK], BF16, name="weight_raw")
+        nc.scalar.dma_start(out=weight_raw[:], in_=gn_weight.rearrange("(c p t) -> p c t", t=PACK, p=P))
+        bias_raw = const.tile([P, PASSES, PACK], BF16, name="bias_raw")
+        nc.scalar.dma_start(out=bias_raw[:], in_=gn_bias.rearrange("(c p t) -> p c t", t=PACK, p=P))
+        weight_col = const.tile([P, K_BLOCKS], F32, name="weight_col")
+        bias_col = const.tile([P, K_BLOCKS], F32, name="bias_col")
+
+        b_all = const.tile([P, E], BF16, name="b_all")
+        nc.scalar.dma_start(out=b_all[:], in_=b_o.partition_broadcast(P))
+
+        def live(r):
+            return 0 <= r < ROUNDS
+
+        first_step = -(AHEAD + 2)
+        for step in range(first_step, ROUNDS + 2):
+            if live(step + AHEAD + 2):
+                load_ret(step + AHEAD + 2)
+            if live(step + 2):
+                load_g(step + 2)
+            if 0 <= step - first_step - 2 < PASSES:
+                load_w(step - first_step - 2)
+
+            if live(step):
+                transpose_r(step, 1)
+            if live(step - 2):
+                matmuls(step - 2, 0)
+                add_bias(step - 2, 0)
+                matmuls(step - 2, 1)
+            if live(step - 1):
+                product(step - 1, 1)
+            if live(step - 2):
+                add_bias(step - 2, 1)
+                store(step - 2)
+            if live(step - 1):
+                quantise(step - 1)
+            if live(step + AHEAD):
+                statistics(step + AHEAD)
+                scale_and_shift(step + AHEAD)
+            if step == -AHEAD:
+                nc.vector.tensor_copy(out=weight_col[:], in_=weight_raw[:].rearrange("p c t -> p (c t)"))
+                nc.vector.tensor_copy(out=bias_col[:], in_=bias_raw[:].rearrange("p c t -> p (c t)"))
+            if 0 <= step + 1 < PASSES:
+                quantise_w(step + 1)
+            if 0 <= step + 2 < PASSES:
+                regroup_w(step + 2)
+
+            if live(step + 1):
+                transpose_g(step + 1, 0)
+                transpose_g(step + 1, 1)
+                normalise(step + 1)
+            if live(step):
+                leave_psum(step, 0)
+            if live(step + 1):
+                transpose_r(step + 1, 0)
+            if live(step):
+                product(step, 0)
+                leave_psum(step, 1)

@@ -20,7 +20,8 @@ HEADS = 4
 HEAD = E // HEADS
 EPS = 1e-5
 PASSES = E // K_PASS
-K_BLOCKS = E // P
+WORDS = E // PACK
+HEAD_WORDS = HEAD // PACK
 TILES = 2
 TOK = TILES * P
 ROUNDS = TOKENS // TOK
@@ -29,7 +30,7 @@ N_BANK = 512
 N_HALVES = E // N_BANK
 RUN = 4
 PAIR = 2
-AHEAD = 3
+AHEAD = 4
 
 FLOPS = 2 * TOKENS * E * E
 
@@ -48,18 +49,19 @@ def tile_multiscaleretention_pc_t_kernel(tc, ret, g, gn_weight, gn_bias, w_o, b_
         g_pool = ctx.enter_context(tc.tile_pool(name="g", bufs=4))
         small = ctx.enter_context(tc.tile_pool(name="small", bufs=AHEAD + 2))
         r_pool = ctx.enter_context(tc.tile_pool(name="r", bufs=3))
-        t_pool = ctx.enter_context(tc.tile_pool(name="transposed", bufs=4))
+        s_pool = ctx.enter_context(tc.tile_pool(name="s", bufs=3))
+        t_pool = ctx.enter_context(tc.tile_pool(name="transposed", bufs=3))
         q_pool = ctx.enter_context(tc.tile_pool(name="quantised", bufs=3))
         o_pool = ctx.enter_context(tc.tile_pool(name="o", bufs=3))
-        psum_r = ctx.enter_context(tc.psum_pool(name="psum_r", bufs=4))
-        psum_g = ctx.enter_context(tc.psum_pool(name="psum_g", bufs=2))
+        psum_r = ctx.enter_context(tc.psum_pool(name="psum_r", bufs=2))
+        psum_s = ctx.enter_context(tc.psum_pool(name="psum_s", bufs=4))
         psum_o = ctx.enter_context(tc.psum_pool(name="psum_o", bufs=2))
         ctx.enter_context(tc.manual_schedule())
 
-        x_of, g_of, stats_of, rstd_of, shift_of, r_of, gate_of, codes_of, scales_of, out_of = (
+        x_of, g_of, stats_of, rstd_of, r_of, s_of, gate_of, codes_of, scales_of, out_of = (
             {}, {}, {}, {}, {}, {}, {}, {}, {}, {},
         )
-        g_bank_of, r_banks_of, silu_of, rn_of, acc_of = {}, {}, {}, {}, {}
+        r_banks_of, s_bank_of, rn_of, acc_of = {}, {}, {}, {}
         w_raw_of, w_grouped_of = {}, {}
 
         def load_ret(r):
@@ -70,69 +72,67 @@ def tile_multiscaleretention_pc_t_kernel(tc, ret, g, gn_weight, gn_bias, w_o, b_
             g_of[r] = g_pool.tile([P, TILES, E], BF16, name="g_sb")
             nc.sync.dma_start(out=g_of[r][:], in_=g_rounds[r])
 
-        def statistics(r):
-            stats = small.tile([P, GROUPS, 3], F32, name="stats")
-            for j in range(TILES):
-                for pair in range(HEADS // 2):
-                    i = j * HEADS + 2 * pair
-                    nc.vector.bn_stats(
-                        out=stats[:, i : i + 2, :].rearrange("p a s -> p (a s)"),
-                        in_=x_of[r][:, j, 2 * pair * HEAD : 2 * (pair + 1) * HEAD].rearrange("p (a d) -> p d a", a=2),
-                    )
-            stats_of[r] = stats
+        def statistics(r, j):
+            if j == 0:
+                stats_of[r] = small.tile([P, GROUPS, 3], F32, name="stats")
+            for pair in range(HEADS // 2):
+                i = j * HEADS + 2 * pair
+                nc.vector.bn_stats(
+                    out=stats_of[r][:, i : i + 2, :].rearrange("p a s -> p (a s)"),
+                    in_=x_of[r][:, j, 2 * pair * HEAD : 2 * (pair + 1) * HEAD].rearrange("p (a d) -> p d a", a=2),
+                )
 
-        def scale_and_shift(r):
-            mean, count_var = stats_of[r][:, :, 1], stats_of[r][:, :, 2]
+        def inverse_deviation(r):
             var_eps = small.tile([P, GROUPS], F32, name="var_eps")
             nc.gpsimd.tensor_scalar(
-                out=var_eps[:], in0=count_var, scalar1=1.0 / HEAD, scalar2=EPS, op0=ALU.mult, op1=ALU.add
+                out=var_eps[:], in0=stats_of[r][:, :, 2], scalar1=1.0 / HEAD, scalar2=EPS, op0=ALU.mult, op1=ALU.add
             )
-            minus_mean = small.tile([P, GROUPS], F32, name="minus_mean")
-            nc.gpsimd.tensor_scalar(out=minus_mean[:], in0=mean, scalar1=-1.0, scalar2=0.0, op0=ALU.mult, op1=ALU.add)
             rstd_of[r] = small.tile([P, GROUPS], F32, name="rstd")
             nc.gpsimd.tensor_tensor(out=rstd_of[r][:], in0=var_eps[:], in1=minus_half[:], op=ALU.pow)
-            shift_of[r] = small.tile([P, GROUPS], F32, name="shift")
-            nc.gpsimd.tensor_tensor(out=shift_of[r][:], in0=minus_mean[:], in1=rstd_of[r][:], op=ALU.mult)
 
         def normalise(r):
-            r_of[r] = r_pool.tile([P, TILES, E], F32, name="r_sb")
+            r_of[r] = r_pool.tile([P, TILES, PACK, WORDS], F32, name="r_sb")
             for j in range(TILES):
                 for h in range(HEADS):
                     i = j * HEADS + h
-                    cols = slice(h * HEAD, (h + 1) * HEAD)
-                    nc.scalar.activation(
-                        out=r_of[r][:, j, cols], in_=x_of[r][:, j, cols], func=ACT.Identity,
-                        scale=rstd_of[r][:, i : i + 1], bias=shift_of[r][:, i : i + 1],
+                    nc.gpsimd.tensor_scalar(
+                        out=r_of[r][:, j, :, h * HEAD_WORDS : (h + 1) * HEAD_WORDS],
+                        in0=x_of[r][:, j, h * HEAD : (h + 1) * HEAD].rearrange("p (k t) -> p t k", t=PACK),
+                        scalar1=stats_of[r][:, i, 1:2],
+                        scalar2=rstd_of[r][:, i : i + 1],
+                        op0=ALU.subtract,
+                        op1=ALU.mult,
                     )
 
-        def transpose_g(r, c):
-            g_bank = psum_g.tile([P, PACK, TOK], BF16, name="g_bank")
-            for t in range(PACK):
-                for j in range(TILES):
-                    nc.tensor.transpose(
-                        g_bank[:, t, j * P : (j + 1) * P],
-                        g_of[r][:, j, c * K_PASS + t : (c + 1) * K_PASS : PACK],
-                        ident_bf16[:],
-                    )
-            g_bank_of[r, c] = g_bank
+        def swish(r, j):
+            if j == 0:
+                s_of[r] = s_pool.tile([P, TILES, PACK, WORDS], F32, name="s_sb")
+            nc.scalar.activation(
+                out=s_of[r][:, j], in_=g_of[r][:, j, :].rearrange("p (k t) -> p t k", t=PACK), func=ACT.Silu
+            )
 
         def transpose_r(r, c):
             r_banks_of[r, c] = []
             for half in range(PACK // 2):
                 r_bank = psum_r.tile([P, 2, TOK], F32, name="r_bank")
                 for i in range(2):
-                    t = 2 * half + i
                     for j in range(TILES):
                         nc.tensor.transpose(
                             r_bank[:, i, j * P : (j + 1) * P],
-                            r_of[r][:, j, c * K_PASS + t : (c + 1) * K_PASS : PACK],
-                            ident_f32[:],
+                            r_of[r][:, j, 2 * half + i, c * P : (c + 1) * P],
+                            ident[:],
                         )
                 r_banks_of[r, c].append(r_bank)
 
-        def leave_psum(r, c):
-            silu_of[r, c] = t_pool.tile([P, PACK, TOK], F32, name="silu_t")
-            nc.scalar.activation(out=silu_of[r, c][:], in_=g_bank_of[r, c][:], func=ACT.Silu)
+        def transpose_s(r, c):
+            for j in range(TILES):
+                s_bank_of[r, c, j] = psum_s.tile([P, PACK, P], F32, name="s_bank")
+                for t in range(PACK):
+                    nc.tensor.transpose(
+                        s_bank_of[r, c, j][:, t, :], s_of[r][:, j, t, c * P : (c + 1) * P], ident[:]
+                    )
+
+        def affine(r, c):
             rn_of[r, c] = t_pool.tile([P, PACK, TOK], F32, name="rn_t")
             for t in range(PACK):
                 m = c * PACK + t
@@ -141,13 +141,14 @@ def tile_multiscaleretention_pc_t_kernel(tc, ret, g, gn_weight, gn_bias, w_o, b_
                     scale=weight_col[:, m : m + 1], bias=bias_col[:, m : m + 1],
                 )
 
-        def product(r, c):
-            if c == 0:
+        def product(r, c, j):
+            if c == 0 and j == 0:
                 gate_of[r] = q_pool.tile([P, PASSES, TOK, PACK], BF16, name="gate", align_bytes=64)
+            tokens = slice(j * P, (j + 1) * P)
             nc.vector.tensor_tensor(
-                out=gate_of[r][:, c].rearrange("p (q i) t -> p q t i", i=PAIR),
-                in0=rn_of[r, c][:].rearrange("p t (q i) -> p q t i", i=PAIR),
-                in1=silu_of[r, c][:].rearrange("p t (q i) -> p q t i", i=PAIR),
+                out=gate_of[r][:, c, tokens, :].rearrange("p (q i) t -> p q t i", i=PAIR),
+                in0=s_bank_of[r, c, j][:].rearrange("p t (q i) -> p q t i", i=PAIR),
+                in1=rn_of[r, c][:, :, tokens].rearrange("p t (q i) -> p q t i", i=PAIR),
                 op=ALU.mult,
             )
 
@@ -206,10 +207,8 @@ def tile_multiscaleretention_pc_t_kernel(tc, ret, g, gn_weight, gn_bias, w_o, b_
                 in_=w_grouped_of[c][:].rearrange("p n t -> p (n t)"),
             )
 
-        ident_f32 = const.tile([P, P], F32, name="ident_f32")
-        make_identity(nc, ident_f32[:])
-        ident_bf16 = const.tile([P, P], BF16, name="ident_bf16")
-        make_identity(nc, ident_bf16[:])
+        ident = const.tile([P, P], F32, name="ident")
+        make_identity(nc, ident[:])
         minus_half = const.tile([P, GROUPS], F32, name="minus_half")
         nc.gpsimd.memset(minus_half[:], -0.5)
         w_codes = const.tile([P, PASSES, E], U32, name="w_codes", align_bytes=64)
@@ -219,8 +218,8 @@ def tile_multiscaleretention_pc_t_kernel(tc, ret, g, gn_weight, gn_bias, w_o, b_
         nc.scalar.dma_start(out=weight_raw[:], in_=gn_weight.rearrange("(c p t) -> p c t", t=PACK, p=P))
         bias_raw = const.tile([P, PASSES, PACK], BF16, name="bias_raw")
         nc.scalar.dma_start(out=bias_raw[:], in_=gn_bias.rearrange("(c p t) -> p c t", t=PACK, p=P))
-        weight_col = const.tile([P, K_BLOCKS], F32, name="weight_col")
-        bias_col = const.tile([P, K_BLOCKS], F32, name="bias_col")
+        weight_col = const.tile([P, PASSES * PACK], F32, name="weight_col")
+        bias_col = const.tile([P, PASSES * PACK], F32, name="bias_col")
 
         b_all = const.tile([P, E], BF16, name="b_all")
         nc.scalar.dma_start(out=b_all[:], in_=b_o.partition_broadcast(P))
@@ -229,46 +228,55 @@ def tile_multiscaleretention_pc_t_kernel(tc, ret, g, gn_weight, gn_bias, w_o, b_
             return 0 <= r < ROUNDS
 
         first_step = -(AHEAD + 2)
-        for step in range(first_step, ROUNDS + 2):
+        for step in range(first_step, ROUNDS + 1):
             if live(step + AHEAD + 2):
                 load_ret(step + AHEAD + 2)
+            if live(step + 4):
+                load_g(step + 4)
+            if 0 <= step - first_step - 3 < PASSES:
+                load_w(step - first_step - 3)
+
+            if live(step + 3):
+                inverse_deviation(step + 3)
             if live(step + 2):
-                load_g(step + 2)
-            if 0 <= step - first_step - 2 < PASSES:
-                load_w(step - first_step - 2)
+                normalise(step + 2)
 
             if live(step):
+                product(step, 0, 0)
+                product(step, 0, 1)
+            if live(step - 1):
+                matmuls(step - 1, 0)
+            if live(step):
                 transpose_r(step, 1)
-            if live(step - 2):
-                matmuls(step - 2, 0)
-                add_bias(step - 2, 0)
-                matmuls(step - 2, 1)
+                transpose_s(step, 1)
+                affine(step, 1)
+            if live(step + 2):
+                swish(step + 2, 0)
             if live(step - 1):
-                product(step - 1, 1)
-            if live(step - 2):
-                add_bias(step - 2, 1)
-                store(step - 2)
+                add_bias(step - 1, 0)
+                matmuls(step - 1, 1)
+            if live(step):
+                product(step, 1, 0)
+                product(step, 1, 1)
+            if live(step + 1):
+                transpose_r(step + 1, 0)
+                transpose_s(step + 1, 0)
+                affine(step + 1, 0)
+            if live(step + 2):
+                swish(step + 2, 1)
             if live(step - 1):
-                quantise(step - 1)
+                add_bias(step - 1, 1)
+                store(step - 1)
             if live(step + AHEAD):
-                statistics(step + AHEAD)
-                scale_and_shift(step + AHEAD)
-            if step == -AHEAD:
+                statistics(step + AHEAD, 0)
+            if live(step):
+                quantise(step)
+            if live(step + AHEAD):
+                statistics(step + AHEAD, 1)
+            if step == -3:
                 nc.vector.tensor_copy(out=weight_col[:], in_=weight_raw[:].rearrange("p c t -> p (c t)"))
                 nc.vector.tensor_copy(out=bias_col[:], in_=bias_raw[:].rearrange("p c t -> p (c t)"))
             if 0 <= step + 1 < PASSES:
                 quantise_w(step + 1)
             if 0 <= step + 2 < PASSES:
                 regroup_w(step + 2)
-
-            if live(step + 1):
-                transpose_g(step + 1, 0)
-                transpose_g(step + 1, 1)
-                normalise(step + 1)
-            if live(step):
-                leave_psum(step, 0)
-            if live(step + 1):
-                transpose_r(step + 1, 0)
-            if live(step):
-                product(step, 0)
-                leave_psum(step, 1)

@@ -30,6 +30,7 @@ N_BANK = 512
 N_HALVES = E // N_BANK
 RUN = 4
 PAIR = 2
+SCALAR_HEADS = 3
 AHEAD = 4
 
 FLOPS = 2 * TOKENS * E * E
@@ -58,8 +59,8 @@ def tile_multiscaleretention_pc_t_kernel(tc, ret, g, gn_weight, gn_bias, w_o, b_
         psum_o = ctx.enter_context(tc.psum_pool(name="psum_o", bufs=2))
         ctx.enter_context(tc.manual_schedule())
 
-        x_of, g_of, stats_of, rstd_of, r_of, s_of, gate_of, codes_of, scales_of, out_of = (
-            {}, {}, {}, {}, {}, {}, {}, {}, {}, {},
+        x_of, g_of, stats_of, rstd_of, shift_of, r_of, s_of, gate_of, codes_of, scales_of, out_of = (
+            {}, {}, {}, {}, {}, {}, {}, {}, {}, {}, {},
         )
         r_banks_of, s_bank_of, rn_of, acc_of = {}, {}, {}, {}
         w_raw_of, w_grouped_of = {}, {}
@@ -89,19 +90,26 @@ def tile_multiscaleretention_pc_t_kernel(tc, ret, g, gn_weight, gn_bias, w_o, b_
             )
             rstd_of[r] = small.tile([P, GROUPS], F32, name="rstd")
             nc.gpsimd.tensor_tensor(out=rstd_of[r][:], in0=var_eps[:], in1=minus_half[:], op=ALU.pow)
+            minus_mean = small.tile([P, GROUPS], F32, name="minus_mean")
+            nc.gpsimd.tensor_scalar(
+                out=minus_mean[:], in0=stats_of[r][:, :, 1], scalar1=-1.0, scalar2=0.0, op0=ALU.mult, op1=ALU.add
+            )
+            shift_of[r] = small.tile([P, GROUPS], F32, name="shift")
+            nc.gpsimd.tensor_tensor(out=shift_of[r][:], in0=minus_mean[:], in1=rstd_of[r][:], op=ALU.mult)
 
-        def normalise(r):
-            r_of[r] = r_pool.tile([P, TILES, PACK, WORDS], F32, name="r_sb")
-            for j in range(TILES):
-                for h in range(HEADS):
-                    i = j * HEADS + h
+        def normalise(r, j):
+            if j == 0:
+                r_of[r] = r_pool.tile([P, TILES, PACK, WORDS], F32, name="r_sb")
+            for h in range(HEADS):
+                i = j * HEADS + h
+                r_head = r_of[r][:, j, :, h * HEAD_WORDS : (h + 1) * HEAD_WORDS]
+                x_head = x_of[r][:, j, h * HEAD : (h + 1) * HEAD].rearrange("p (k t) -> p t k", t=PACK)
+                rstd, shift = rstd_of[r][:, i : i + 1], shift_of[r][:, i : i + 1]
+                if h < SCALAR_HEADS:
+                    nc.scalar.activation(out=r_head, in_=x_head, func=ACT.Identity, scale=rstd, bias=shift)
+                else:
                     nc.gpsimd.tensor_scalar(
-                        out=r_of[r][:, j, :, h * HEAD_WORDS : (h + 1) * HEAD_WORDS],
-                        in0=x_of[r][:, j, h * HEAD : (h + 1) * HEAD].rearrange("p (k t) -> p t k", t=PACK),
-                        scalar1=stats_of[r][:, i, 1:2],
-                        scalar2=rstd_of[r][:, i : i + 1],
-                        op0=ALU.subtract,
-                        op1=ALU.mult,
+                        out=r_head, in0=x_head, scalar1=rstd, scalar2=shift, op0=ALU.mult, op1=ALU.add
                     )
 
         def swish(r, j):
@@ -238,8 +246,6 @@ def tile_multiscaleretention_pc_t_kernel(tc, ret, g, gn_weight, gn_bias, w_o, b_
 
             if live(step + 3):
                 inverse_deviation(step + 3)
-            if live(step + 2):
-                normalise(step + 2)
 
             if live(step):
                 product(step, 0, 0)
@@ -252,6 +258,7 @@ def tile_multiscaleretention_pc_t_kernel(tc, ret, g, gn_weight, gn_bias, w_o, b_
                 affine(step, 1)
             if live(step + 2):
                 swish(step + 2, 0)
+                normalise(step + 2, 0)
             if live(step - 1):
                 add_bias(step - 1, 0)
                 matmuls(step - 1, 1)
@@ -264,6 +271,7 @@ def tile_multiscaleretention_pc_t_kernel(tc, ret, g, gn_weight, gn_bias, w_o, b_
                 affine(step + 1, 0)
             if live(step + 2):
                 swish(step + 2, 1)
+                normalise(step + 2, 1)
             if live(step - 1):
                 add_bias(step - 1, 1)
                 store(step - 1)

@@ -73,15 +73,14 @@ def tile_multiscaleretention_pc_t_kernel(tc, ret, g, gn_weight, gn_bias, w_o, b_
             g_of[r] = g_pool.tile([P, TILES, E], BF16, name="g_sb")
             nc.sync.dma_start(out=g_of[r][:], in_=g_rounds[r])
 
-        def statistics(r, j):
-            if j == 0:
+        def statistics(r, j, pair):
+            if j == 0 and pair == 0:
                 stats_of[r] = small.tile([P, GROUPS, 3], F32, name="stats")
-            for pair in range(HEADS // 2):
-                i = j * HEADS + 2 * pair
-                nc.vector.bn_stats(
-                    out=stats_of[r][:, i : i + 2, :].rearrange("p a s -> p (a s)"),
-                    in_=x_of[r][:, j, 2 * pair * HEAD : 2 * (pair + 1) * HEAD].rearrange("p (a d) -> p d a", a=2),
-                )
+            i = j * HEADS + 2 * pair
+            nc.vector.bn_stats(
+                out=stats_of[r][:, i : i + 2, :].rearrange("p a s -> p (a s)"),
+                in_=x_of[r][:, j, 2 * pair * HEAD : 2 * (pair + 1) * HEAD].rearrange("p (a d) -> p d a", a=2),
+            )
 
         def inverse_deviation(r):
             var_eps = small.tile([P, GROUPS], F32, name="var_eps")
@@ -169,30 +168,28 @@ def tile_multiscaleretention_pc_t_kernel(tc, ret, g, gn_weight, gn_bias, w_o, b_
                 in_=gate_of[r][:].rearrange("p c k t -> p (c k t)"),
             )
 
-        def matmuls(r, j):
+        def matmuls(r, j, n):
             tokens = slice(j * P, (j + 1) * P)
-            for n in range(N_HALVES):
-                n_cols = slice(n * N_BANK, (n + 1) * N_BANK)
-                acc_of[r, j, n] = psum_o.tile([P, N_BANK], F32, name="acc")
-                for c in range(PASSES):
-                    nc.tensor.matmul_mx(
-                        out=acc_of[r, j, n][:],
-                        lhsT=codes_of[r][:, c, tokens].bitcast(FP8X4),
-                        lhsT_scale=scales_of[r][:, c, tokens],
-                        rhs=w_codes[:, c, n_cols].bitcast(FP8X4),
-                        rhs_scale=w_scales[:, c, n_cols],
-                        start=(c == 0),
-                        stop=(c == PASSES - 1),
-                    )
-
-        def add_bias(r, j):
-            if j == 0:
-                out_of[r] = o_pool.tile([P, TILES, E], F32, name="out_sb")
-            for n in range(N_HALVES):
-                n_cols = slice(n * N_BANK, (n + 1) * N_BANK)
-                nc.vector.tensor_tensor(
-                    out=out_of[r][:, j, n_cols], in0=acc_of[r, j, n][:], in1=b_all[:, n_cols], op=ALU.add
+            n_cols = slice(n * N_BANK, (n + 1) * N_BANK)
+            acc_of[r, j, n] = psum_o.tile([P, N_BANK], F32, name="acc")
+            for c in range(PASSES):
+                nc.tensor.matmul_mx(
+                    out=acc_of[r, j, n][:],
+                    lhsT=codes_of[r][:, c, tokens].bitcast(FP8X4),
+                    lhsT_scale=scales_of[r][:, c, tokens],
+                    rhs=w_codes[:, c, n_cols].bitcast(FP8X4),
+                    rhs_scale=w_scales[:, c, n_cols],
+                    start=(c == 0),
+                    stop=(c == PASSES - 1),
                 )
+
+        def add_bias(r, j, n):
+            if j == 0 and n == 0:
+                out_of[r] = o_pool.tile([P, TILES, E], F32, name="out_sb")
+            n_cols = slice(n * N_BANK, (n + 1) * N_BANK)
+            nc.vector.tensor_tensor(
+                out=out_of[r][:, j, n_cols], in0=acc_of[r, j, n][:], in1=b_all[:, n_cols], op=ALU.add
+            )
 
         def store(r):
             nc.sync.dma_start(out=out_rounds[r], in_=out_of[r][:])
@@ -247,40 +244,30 @@ def tile_multiscaleretention_pc_t_kernel(tc, ret, g, gn_weight, gn_bias, w_o, b_
             if live(step + 3):
                 inverse_deviation(step + 3)
 
-            if live(step):
-                product(step, 0, 0)
-                product(step, 0, 1)
+            for j in range(TILES):
+                for n in range(N_HALVES):
+                    if live(step - 1):
+                        matmuls(step - 1, j, n)
+                    t_round, t_pass = (step, 1) if j == 0 else (step + 1, 0)
+                    if live(t_round):
+                        if n == 0:
+                            transpose_r(t_round, t_pass)
+                            affine(t_round, t_pass)
+                        else:
+                            transpose_s(t_round, t_pass)
+                    if live(step):
+                        product(step, j, n)
+                    if live(step - 1):
+                        add_bias(step - 1, j, n)
+                    if live(step) and (j, n) == (TILES - 1, N_HALVES - 1):
+                        quantise(step)
+                    if live(step + AHEAD):
+                        statistics(step + AHEAD, j, n)
+                if live(step + 2):
+                    swish(step + 2, j)
+                    normalise(step + 2, j)
             if live(step - 1):
-                matmuls(step - 1, 0)
-            if live(step):
-                transpose_r(step, 1)
-                transpose_s(step, 1)
-                affine(step, 1)
-            if live(step + 2):
-                swish(step + 2, 0)
-                normalise(step + 2, 0)
-            if live(step - 1):
-                add_bias(step - 1, 0)
-                matmuls(step - 1, 1)
-            if live(step):
-                product(step, 1, 0)
-                product(step, 1, 1)
-            if live(step + 1):
-                transpose_r(step + 1, 0)
-                transpose_s(step + 1, 0)
-                affine(step + 1, 0)
-            if live(step + 2):
-                swish(step + 2, 1)
-                normalise(step + 2, 1)
-            if live(step - 1):
-                add_bias(step - 1, 1)
                 store(step - 1)
-            if live(step + AHEAD):
-                statistics(step + AHEAD, 0)
-            if live(step):
-                quantise(step)
-            if live(step + AHEAD):
-                statistics(step + AHEAD, 1)
             if step == -3:
                 nc.vector.tensor_copy(out=weight_col[:], in_=weight_raw[:].rearrange("p c t -> p (c t)"))
                 nc.vector.tensor_copy(out=bias_col[:], in_=bias_raw[:].rearrange("p c t -> p (c t)"))

@@ -31,7 +31,9 @@ N_HALVES = E // N_BANK
 RUN = 4
 PAIR = 2
 SCALAR_HEADS = 3
-AHEAD = 4
+QUARTERS = [(0, 0), (0, 1), (1, 0), (1, 1)]
+POOL_QUARTER = (0, 0)
+AHEAD = 3
 
 FLOPS = 2 * TOKENS * E * E
 
@@ -50,13 +52,13 @@ def tile_multiscaleretention_pc_t_kernel(tc, ret, g, gn_weight, gn_bias, w_o, b_
         g_pool = ctx.enter_context(tc.tile_pool(name="g", bufs=4))
         small = ctx.enter_context(tc.tile_pool(name="small", bufs=AHEAD + 2))
         r_pool = ctx.enter_context(tc.tile_pool(name="r", bufs=3))
-        s_pool = ctx.enter_context(tc.tile_pool(name="s", bufs=3))
+        s_pool = ctx.enter_context(tc.tile_pool(name="s", bufs=4))
         t_pool = ctx.enter_context(tc.tile_pool(name="transposed", bufs=3))
         q_pool = ctx.enter_context(tc.tile_pool(name="quantised", bufs=3))
         o_pool = ctx.enter_context(tc.tile_pool(name="o", bufs=3))
         psum_r = ctx.enter_context(tc.psum_pool(name="psum_r", bufs=2))
-        psum_s = ctx.enter_context(tc.psum_pool(name="psum_s", bufs=4))
-        psum_o = ctx.enter_context(tc.psum_pool(name="psum_o", bufs=2))
+        psum_s = ctx.enter_context(tc.psum_pool(name="psum_s", bufs=3))
+        psum_o = ctx.enter_context(tc.psum_pool(name="psum_o", bufs=3))
         ctx.enter_context(tc.manual_schedule())
 
         x_of, g_of, stats_of, rstd_of, shift_of, r_of, s_of, gate_of, codes_of, scales_of, out_of = (
@@ -171,6 +173,8 @@ def tile_multiscaleretention_pc_t_kernel(tc, ret, g, gn_weight, gn_bias, w_o, b_
         def matmuls(r, j, n):
             tokens = slice(j * P, (j + 1) * P)
             n_cols = slice(n * N_BANK, (n + 1) * N_BANK)
+            if j == 0 and n == 0:
+                out_of[r] = o_pool.tile([P, TILES, E], F32, name="out_sb")
             acc_of[r, j, n] = psum_o.tile([P, N_BANK], F32, name="acc")
             for c in range(PASSES):
                 nc.tensor.matmul_mx(
@@ -184,11 +188,19 @@ def tile_multiscaleretention_pc_t_kernel(tc, ret, g, gn_weight, gn_bias, w_o, b_
                 )
 
         def add_bias(r, j, n):
-            if j == 0 and n == 0:
-                out_of[r] = o_pool.tile([P, TILES, E], F32, name="out_sb")
             n_cols = slice(n * N_BANK, (n + 1) * N_BANK)
             nc.vector.tensor_tensor(
                 out=out_of[r][:, j, n_cols], in0=acc_of[r, j, n][:], in1=b_all[:, n_cols], op=ALU.add
+            )
+
+        def empty_bank(r, j, n):
+            n_cols = slice(n * N_BANK, (n + 1) * N_BANK)
+            nc.scalar.activation(out=out_of[r][:, j, n_cols], in_=acc_of[r, j, n][:], func=ACT.Identity)
+
+        def add_bias_in_sbuf(r, j, n):
+            n_cols = slice(n * N_BANK, (n + 1) * N_BANK)
+            nc.gpsimd.tensor_tensor(
+                out=out_of[r][:, j, n_cols], in0=out_of[r][:, j, n_cols], in1=b_all[:, n_cols], op=ALU.add
             )
 
         def store(r):
@@ -232,22 +244,20 @@ def tile_multiscaleretention_pc_t_kernel(tc, ret, g, gn_weight, gn_bias, w_o, b_
         def live(r):
             return 0 <= r < ROUNDS
 
-        first_step = -(AHEAD + 2)
-        for step in range(first_step, ROUNDS + 1):
+        first_step = -5
+        for step in range(first_step, ROUNDS + 2):
             if live(step + AHEAD + 2):
                 load_ret(step + AHEAD + 2)
-            if live(step + 4):
-                load_g(step + 4)
-            if 0 <= step - first_step - 3 < PASSES:
-                load_w(step - first_step - 3)
+            if live(step + 5):
+                load_g(step + 5)
+            if 0 <= step - (-4) < PASSES:
+                load_w(step - (-4))
 
-            if live(step + 3):
-                inverse_deviation(step + 3)
+            if live(step + 2):
+                inverse_deviation(step + 2)
 
             for j in range(TILES):
                 for n in range(N_HALVES):
-                    if live(step - 1):
-                        matmuls(step - 1, j, n)
                     t_round, t_pass = (step, 1) if j == 0 else (step + 1, 0)
                     if live(t_round):
                         if n == 0:
@@ -255,23 +265,33 @@ def tile_multiscaleretention_pc_t_kernel(tc, ret, g, gn_weight, gn_bias, w_o, b_
                             affine(t_round, t_pass)
                         else:
                             transpose_s(t_round, t_pass)
+                    if live(step - 1):
+                        matmuls(step - 1, j, n)
+                    if live(step - 1) and (j, n) == POOL_QUARTER:
+                        empty_bank(step - 1, j, n)
                     if live(step):
                         product(step, j, n)
-                    if live(step - 1):
-                        add_bias(step - 1, j, n)
+                    b_round = step - 1 if (j, n) != QUARTERS[0] else step - 2
+                    b_quarter = QUARTERS[QUARTERS.index((j, n)) - 1]
+                    if live(b_round):
+                        if b_quarter == POOL_QUARTER:
+                            add_bias_in_sbuf(b_round, *b_quarter)
+                        else:
+                            add_bias(b_round, *b_quarter)
+                        if b_quarter == QUARTERS[-1]:
+                            store(b_round)
                     if live(step) and (j, n) == (TILES - 1, N_HALVES - 1):
                         quantise(step)
                     if live(step + AHEAD):
                         statistics(step + AHEAD, j, n)
+                if live(step + 3):
+                    swish(step + 3, j)
                 if live(step + 2):
-                    swish(step + 2, j)
                     normalise(step + 2, j)
-            if live(step - 1):
-                store(step - 1)
             if step == -3:
                 nc.vector.tensor_copy(out=weight_col[:], in_=weight_raw[:].rearrange("p c t -> p (c t)"))
                 nc.vector.tensor_copy(out=bias_col[:], in_=bias_raw[:].rearrange("p c t -> p (c t)"))
-            if 0 <= step + 1 < PASSES:
-                quantise_w(step + 1)
-            if 0 <= step + 2 < PASSES:
-                regroup_w(step + 2)
+            if 0 <= step - (-1) < PASSES:
+                quantise_w(step - (-1))
+            if 0 <= step - (-2) < PASSES:
+                regroup_w(step - (-2))

@@ -30,10 +30,10 @@ N_BANK = 512
 N_HALVES = E // N_BANK
 RUN = 4
 PAIR = 2
-SCALAR_HEADS = 3
+SCALAR_HEADS = 2
 QUARTERS = [(0, 0), (0, 1), (1, 0), (1, 1)]
 POOL_QUARTER = (0, 0)
-AHEAD = 3
+AHEAD = 4
 
 FLOPS = 2 * TOKENS * E * E
 
@@ -244,7 +244,7 @@ def tile_multiscaleretention_pc_t_kernel(tc, ret, g, gn_weight, gn_bias, w_o, b_
         def live(r):
             return 0 <= r < ROUNDS
 
-        first_step = -5
+        first_step = -6
         for step in range(first_step, ROUNDS + 2):
             if live(step + AHEAD + 2):
                 load_ret(step + AHEAD + 2)
@@ -253,8 +253,8 @@ def tile_multiscaleretention_pc_t_kernel(tc, ret, g, gn_weight, gn_bias, w_o, b_
             if 0 <= step - (-4) < PASSES:
                 load_w(step - (-4))
 
-            if live(step + 2):
-                inverse_deviation(step + 2)
+            if live(step + 3):
+                inverse_deviation(step + 3)
 
             for j in range(TILES):
                 for n in range(N_HALVES):

@@ -30,7 +30,7 @@ N_BANK = 512
 N_HALVES = E // N_BANK
 RUN = 4
 PAIR = 2
-SCALAR_HEADS = 2
+SCALAR_HEADS = (2, 3)
 QUARTERS = [(0, 0), (0, 1), (1, 0), (1, 1)]
 POOL_QUARTER = (0, 0)
 AHEAD = 4
@@ -53,7 +53,7 @@ def tile_multiscaleretention_pc_t_kernel(tc, ret, g, gn_weight, gn_bias, w_o, b_
         small = ctx.enter_context(tc.tile_pool(name="small", bufs=AHEAD + 2))
         r_pool = ctx.enter_context(tc.tile_pool(name="r", bufs=3))
         s_pool = ctx.enter_context(tc.tile_pool(name="s", bufs=4))
-        t_pool = ctx.enter_context(tc.tile_pool(name="transposed", bufs=3))
+        t_pool = ctx.enter_context(tc.tile_pool(name="transposed", bufs=4))
         q_pool = ctx.enter_context(tc.tile_pool(name="quantised", bufs=3))
         o_pool = ctx.enter_context(tc.tile_pool(name="o", bufs=3))
         psum_r = ctx.enter_context(tc.psum_pool(name="psum_r", bufs=2))
@@ -106,7 +106,7 @@ def tile_multiscaleretention_pc_t_kernel(tc, ret, g, gn_weight, gn_bias, w_o, b_
                 r_head = r_of[r][:, j, :, h * HEAD_WORDS : (h + 1) * HEAD_WORDS]
                 x_head = x_of[r][:, j, h * HEAD : (h + 1) * HEAD].rearrange("p (k t) -> p t k", t=PACK)
                 rstd, shift = rstd_of[r][:, i : i + 1], shift_of[r][:, i : i + 1]
-                if h < SCALAR_HEADS:
+                if h < SCALAR_HEADS[j]:
                     nc.scalar.activation(out=r_head, in_=x_head, func=ACT.Identity, scale=rstd, bias=shift)
                 else:
                     nc.gpsimd.tensor_scalar(
@@ -258,13 +258,12 @@ def tile_multiscaleretention_pc_t_kernel(tc, ret, g, gn_weight, gn_bias, w_o, b_
 
             for j in range(TILES):
                 for n in range(N_HALVES):
-                    t_round, t_pass = (step, 1) if j == 0 else (step + 1, 0)
-                    if live(t_round):
-                        if n == 0:
-                            transpose_r(t_round, t_pass)
-                            affine(t_round, t_pass)
-                        else:
-                            transpose_s(t_round, t_pass)
+                    if n == 0 and live(step + 1):
+                        transpose_r(step + 1, j)
+                        affine(step + 1, j)
+                    s_round, s_pass = (step, 1) if j == 0 else (step + 1, 0)
+                    if n == 1 and live(s_round):
+                        transpose_s(s_round, s_pass)
                     if live(step - 1):
                         matmuls(step - 1, j, n)
                     if live(step - 1) and (j, n) == POOL_QUARTER:
@@ -284,10 +283,12 @@ def tile_multiscaleretention_pc_t_kernel(tc, ret, g, gn_weight, gn_bias, w_o, b_
                         quantise(step)
                     if live(step + AHEAD):
                         statistics(step + AHEAD, j, n)
-                if live(step + 3):
-                    swish(step + 3, j)
-                if live(step + 2):
-                    normalise(step + 2, j)
+                if j == 0 and live(step + 2):
+                    normalise(step + 2, 0)
+                    normalise(step + 2, 1)
+                if j == 1 and live(step + 3):
+                    swish(step + 3, 0)
+                    swish(step + 3, 1)
             if step == -3:
                 nc.vector.tensor_copy(out=weight_col[:], in_=weight_raw[:].rearrange("p c t -> p (c t)"))
                 nc.vector.tensor_copy(out=bias_col[:], in_=bias_raw[:].rearrange("p c t -> p (c t)"))

@@ -69,7 +69,11 @@ def tile_multiscaleretention_pc_t_kernel(tc, ret, g, gn_weight, gn_bias, w_o, b_
 
         def load_ret(r):
             x_of[r] = x_pool.tile([P, TILES, E], BF16, name="x_sb")
-            nc.sync.dma_start(out=x_of[r][:], in_=ret_rounds[r])
+            if r == 0:
+                for j in range(TILES):
+                    nc.sync.dma_start(out=x_of[r][:, j, :], in_=ret_rounds[r][:, j, :])
+            else:
+                nc.sync.dma_start(out=x_of[r][:], in_=ret_rounds[r])
 
         def load_g(r):
             g_of[r] = g_pool.tile([P, TILES, E], BF16, name="g_sb")
@@ -206,6 +210,10 @@ def tile_multiscaleretention_pc_t_kernel(tc, ret, g, gn_weight, gn_bias, w_o, b_
         def store(r):
             nc.sync.dma_start(out=out_rounds[r], in_=out_of[r][:])
 
+        def store_quarter(r, j, n):
+            n_cols = slice(n * N_BANK, (n + 1) * N_BANK)
+            nc.sync.dma_start(out=out_rounds[r][:, j, n_cols], in_=out_of[r][:, j, n_cols])
+
         def load_w(c):
             w_raw_of[c] = w_stage.tile([P, PACK, E], BF16, name="w_raw")
             nc.sync.dma_start(out=w_raw_of[c][:], in_=w_passes[c])
@@ -232,14 +240,11 @@ def tile_multiscaleretention_pc_t_kernel(tc, ret, g, gn_weight, gn_bias, w_o, b_
         w_scales = const.tile([P, PASSES, E], U8, name="w_scales", align_bytes=64)
 
         weight_raw = const.tile([P, PASSES, PACK], BF16, name="weight_raw")
-        nc.scalar.dma_start(out=weight_raw[:], in_=gn_weight.rearrange("(c p t) -> p c t", t=PACK, p=P))
         bias_raw = const.tile([P, PASSES, PACK], BF16, name="bias_raw")
-        nc.scalar.dma_start(out=bias_raw[:], in_=gn_bias.rearrange("(c p t) -> p c t", t=PACK, p=P))
         weight_col = const.tile([P, PASSES * PACK], F32, name="weight_col")
         bias_col = const.tile([P, PASSES * PACK], F32, name="bias_col")
 
         b_all = const.tile([P, E], BF16, name="b_all")
-        nc.scalar.dma_start(out=b_all[:], in_=b_o.partition_broadcast(P))
 
         def live(r):
             return 0 <= r < ROUNDS
@@ -250,8 +255,13 @@ def tile_multiscaleretention_pc_t_kernel(tc, ret, g, gn_weight, gn_bias, w_o, b_
                 load_ret(step + AHEAD + 2)
             if live(step + 5):
                 load_g(step + 5)
-            if 0 <= step - (-4) < PASSES:
-                load_w(step - (-4))
+            if step == first_step + 1:
+                nc.sync.dma_start(out=weight_raw[:], in_=gn_weight.rearrange("(c p t) -> p c t", t=PACK, p=P))
+                nc.sync.dma_start(out=bias_raw[:], in_=gn_bias.rearrange("(c p t) -> p c t", t=PACK, p=P))
+            if 0 <= step - (first_step + 2) < PASSES:
+                load_w(step - (first_step + 2))
+            if step == first_step + 4:
+                nc.sync.dma_start(out=b_all[:], in_=b_o.partition_broadcast(P))
 
             if live(step + 3):
                 inverse_deviation(step + 3)
@@ -277,7 +287,9 @@ def tile_multiscaleretention_pc_t_kernel(tc, ret, g, gn_weight, gn_bias, w_o, b_
                             add_bias_in_sbuf(b_round, *b_quarter)
                         else:
                             add_bias(b_round, *b_quarter)
-                        if b_quarter == QUARTERS[-1]:
+                        if b_round == ROUNDS - 1:
+                            store_quarter(b_round, *b_quarter)
+                        elif b_quarter == QUARTERS[-1]:
                             store(b_round)
                     if live(step) and (j, n) == (TILES - 1, N_HALVES - 1):
                         quantise(step)

@@ -32,7 +32,6 @@ RUN = 4
 PAIR = 2
 SCALAR_HEADS = (2, 3)
 QUARTERS = [(0, 0), (0, 1), (1, 0), (1, 1)]
-POOL_QUARTER = (0, 0)
 AHEAD = 4
 
 FLOPS = 2 * TOKENS * E * E
@@ -117,11 +116,10 @@ def tile_multiscaleretention_pc_t_kernel(tc, ret, g, gn_weight, gn_bias, w_o, b_
                         out=r_head, in0=x_head, scalar1=rstd, scalar2=shift, op0=ALU.mult, op1=ALU.add
                     )
 
-        def swish(r, j):
-            if j == 0:
-                s_of[r] = s_pool.tile([P, TILES, PACK, WORDS], F32, name="s_sb")
+        def swish(r):
+            s_of[r] = s_pool.tile([P, TILES, PACK, WORDS], F32, name="s_sb")
             nc.scalar.activation(
-                out=s_of[r][:, j], in_=g_of[r][:, j, :].rearrange("p (k t) -> p t k", t=PACK), func=ACT.Silu
+                out=s_of[r][:], in_=g_of[r][:].rearrange("p j (k t) -> p j t k", t=PACK), func=ACT.Silu
             )
 
         def transpose_r(r, c):
@@ -160,8 +158,8 @@ def tile_multiscaleretention_pc_t_kernel(tc, ret, g, gn_weight, gn_bias, w_o, b_
             tokens = slice(j * P, (j + 1) * P)
             nc.vector.tensor_tensor(
                 out=gate_of[r][:, c, tokens, :].rearrange("p (q i) t -> p q t i", i=PAIR),
-                in0=s_bank_of[r, c, j][:].rearrange("p t (q i) -> p q t i", i=PAIR),
-                in1=rn_of[r, c][:, :, tokens].rearrange("p t (q i) -> p q t i", i=PAIR),
+                in0=rn_of[r, c][:, :, tokens].rearrange("p t (q i) -> p q t i", i=PAIR),
+                in1=s_bank_of[r, c, j][:].rearrange("p t (q i) -> p q t i", i=PAIR),
                 op=ALU.mult,
             )
 
@@ -194,7 +192,7 @@ def tile_multiscaleretention_pc_t_kernel(tc, ret, g, gn_weight, gn_bias, w_o, b_
         def add_bias(r, j, n):
             n_cols = slice(n * N_BANK, (n + 1) * N_BANK)
             nc.vector.tensor_tensor(
-                out=out_of[r][:, j, n_cols], in0=acc_of[r, j, n][:], in1=b_all[:, n_cols], op=ALU.add
+                out=out_of[r][:, j, n_cols], in0=b_all[:, n_cols], in1=acc_of[r, j, n][:], op=ALU.add
             )
 
         def empty_bank(r, j, n):
@@ -246,6 +244,9 @@ def tile_multiscaleretention_pc_t_kernel(tc, ret, g, gn_weight, gn_bias, w_o, b_
 
         b_all = const.tile([P, E], BF16, name="b_all")
 
+        def pool_quarters(r):
+            return QUARTERS[:1] if r < ROUNDS - 1 else []
+
         def live(r):
             return 0 <= r < ROUNDS
 
@@ -276,14 +277,14 @@ def tile_multiscaleretention_pc_t_kernel(tc, ret, g, gn_weight, gn_bias, w_o, b_
                         transpose_s(s_round, s_pass)
                     if live(step - 1):
                         matmuls(step - 1, j, n)
-                    if live(step - 1) and (j, n) == POOL_QUARTER:
+                    if live(step - 1) and (j, n) in pool_quarters(step - 1):
                         empty_bank(step - 1, j, n)
                     if live(step):
                         product(step, j, n)
                     b_round = step - 1 if (j, n) != QUARTERS[0] else step - 2
                     b_quarter = QUARTERS[QUARTERS.index((j, n)) - 1]
                     if live(b_round):
-                        if b_quarter == POOL_QUARTER:
+                        if b_quarter in pool_quarters(b_round):
                             add_bias_in_sbuf(b_round, *b_quarter)
                         else:
                             add_bias(b_round, *b_quarter)
@@ -299,8 +300,7 @@ def tile_multiscaleretention_pc_t_kernel(tc, ret, g, gn_weight, gn_bias, w_o, b_
                     normalise(step + 2, 0)
                     normalise(step + 2, 1)
                 if j == 1 and live(step + 3):
-                    swish(step + 3, 0)
-                    swish(step + 3, 1)
+                    swish(step + 3)
             if step == -3:
                 nc.vector.tensor_copy(out=weight_col[:], in_=weight_raw[:].rearrange("p c t -> p (c t)"))
                 nc.vector.tensor_copy(out=bias_col[:], in_=bias_raw[:].rearrange("p c t -> p (c t)"))

@@ -29,7 +29,7 @@ GROUPS = TILES * HEADS
 N_BANK = 512
 N_HALVES = E // N_BANK
 RUN = 4
-PAIR = 2
+PAIR = 4
 SCALAR_HEADS = (2, 3)
 QUARTERS = [(0, 0), (0, 1), (1, 0), (1, 1)]
 AHEAD = 4

from contextlib import ExitStack

import concourse.mybir as mybir
from concourse.masks import make_identity

F32 = mybir.dt.float32
BF16 = mybir.dt.bfloat16
U32 = mybir.dt.uint32
U8 = mybir.dt.uint8
FP8X4 = mybir.dt.float8_e4m3fn_x4
ALU = mybir.AluOpType
ACT = mybir.ActivationFunctionType

P = 128
PACK = 4
K_PASS = P * PACK
TOKENS = 4 * 1024
E = 1024
HEADS = 4
HEAD = E // HEADS
EPS = 1e-5
PASSES = E // K_PASS
WORDS = E // PACK
HEAD_WORDS = HEAD // PACK
TILES = 2
TOK = TILES * P
ROUNDS = TOKENS // TOK
GROUPS = TILES * HEADS
N_BANK = 512
N_HALVES = E // N_BANK
RUN = 4
PAIR = 4
SCALAR_HEADS = (2, 3)
QUARTERS = [(0, 0), (0, 1), (1, 0), (1, 1)]
AHEAD = 4

FLOPS = 2 * TOKENS * E * E


def tile_multiscaleretention_pc_t_kernel(tc, ret, g, gn_weight, gn_bias, w_o, b_o, out):
    nc = tc.nc
    ret_rounds = ret.flatten_outer_dims().rearrange("(r p j) c -> r p j c", p=P, j=TILES)
    g_rounds = g.flatten_outer_dims().rearrange("(r p j) c -> r p j c", p=P, j=TILES)
    out_rounds = out.flatten_outer_dims().rearrange("(r p j) c -> r p j c", p=P, j=TILES)
    w_passes = w_o.rearrange("(c p t) n -> c p t n", t=PACK, p=P)

    with ExitStack() as ctx:
        const = ctx.enter_context(tc.tile_pool(name="const", bufs=1))
        w_stage = ctx.enter_context(tc.tile_pool(name="w_stage", bufs=2))
        x_pool = ctx.enter_context(tc.tile_pool(name="x", bufs=AHEAD + 3))
        g_pool = ctx.enter_context(tc.tile_pool(name="g", bufs=4))
        small = ctx.enter_context(tc.tile_pool(name="small", bufs=AHEAD + 2))
        r_pool = ctx.enter_context(tc.tile_pool(name="r", bufs=3))
        s_pool = ctx.enter_context(tc.tile_pool(name="s", bufs=4))
        t_pool = ctx.enter_context(tc.tile_pool(name="transposed", bufs=4))
        q_pool = ctx.enter_context(tc.tile_pool(name="quantised", bufs=3))
        o_pool = ctx.enter_context(tc.tile_pool(name="o", bufs=3))
        psum_r = ctx.enter_context(tc.psum_pool(name="psum_r", bufs=2))
        psum_s = ctx.enter_context(tc.psum_pool(name="psum_s", bufs=3))
        psum_o = ctx.enter_context(tc.psum_pool(name="psum_o", bufs=3))
        ctx.enter_context(tc.manual_schedule())

        x_of, g_of, stats_of, rstd_of, shift_of, r_of, s_of, gate_of, codes_of, scales_of, out_of = (
            {}, {}, {}, {}, {}, {}, {}, {}, {}, {}, {},
        )
        r_banks_of, s_bank_of, rn_of, acc_of = {}, {}, {}, {}
        w_raw_of, w_grouped_of = {}, {}

        def load_ret(r):
            x_of[r] = x_pool.tile([P, TILES, E], BF16, name="x_sb")
            if r == 0:
                for j in range(TILES):
                    nc.sync.dma_start(out=x_of[r][:, j, :], in_=ret_rounds[r][:, j, :])
            else:
                nc.sync.dma_start(out=x_of[r][:], in_=ret_rounds[r])

        def load_g(r):
            g_of[r] = g_pool.tile([P, TILES, E], BF16, name="g_sb")
            nc.sync.dma_start(out=g_of[r][:], in_=g_rounds[r])

        def statistics(r, j, pair):
            if j == 0 and pair == 0:
                stats_of[r] = small.tile([P, GROUPS, 3], F32, name="stats")
            i = j * HEADS + 2 * pair
            nc.vector.bn_stats(
                out=stats_of[r][:, i : i + 2, :].rearrange("p a s -> p (a s)"),
                in_=x_of[r][:, j, 2 * pair * HEAD : 2 * (pair + 1) * HEAD].rearrange("p (a d) -> p d a", a=2),
            )

        def inverse_deviation(r):
            var_eps = small.tile([P, GROUPS], F32, name="var_eps")
            nc.gpsimd.tensor_scalar(
                out=var_eps[:], in0=stats_of[r][:, :, 2], scalar1=1.0 / HEAD, scalar2=EPS, op0=ALU.mult, op1=ALU.add
            )
            rstd_of[r] = small.tile([P, GROUPS], F32, name="rstd")
            nc.gpsimd.tensor_tensor(out=rstd_of[r][:], in0=var_eps[:], in1=minus_half[:], op=ALU.pow)
            minus_mean = small.tile([P, GROUPS], F32, name="minus_mean")
            nc.gpsimd.tensor_scalar(
                out=minus_mean[:], in0=stats_of[r][:, :, 1], scalar1=-1.0, scalar2=0.0, op0=ALU.mult, op1=ALU.add
            )
            shift_of[r] = small.tile([P, GROUPS], F32, name="shift")
            nc.gpsimd.tensor_tensor(out=shift_of[r][:], in0=minus_mean[:], in1=rstd_of[r][:], op=ALU.mult)

        def normalise(r, j):
            if j == 0:
                r_of[r] = r_pool.tile([P, TILES, PACK, WORDS], F32, name="r_sb")
            for h in range(HEADS):
                i = j * HEADS + h
                r_head = r_of[r][:, j, :, h * HEAD_WORDS : (h + 1) * HEAD_WORDS]
                x_head = x_of[r][:, j, h * HEAD : (h + 1) * HEAD].rearrange("p (k t) -> p t k", t=PACK)
                rstd, shift = rstd_of[r][:, i : i + 1], shift_of[r][:, i : i + 1]
                if h < SCALAR_HEADS[j]:
                    nc.scalar.activation(out=r_head, in_=x_head, func=ACT.Identity, scale=rstd, bias=shift)
                else:
                    nc.gpsimd.tensor_scalar(
                        out=r_head, in0=x_head, scalar1=rstd, scalar2=shift, op0=ALU.mult, op1=ALU.add
                    )

        def swish(r):
            s_of[r] = s_pool.tile([P, TILES, PACK, WORDS], F32, name="s_sb")
            nc.scalar.activation(
                out=s_of[r][:], in_=g_of[r][:].rearrange("p j (k t) -> p j t k", t=PACK), func=ACT.Silu
            )

        def transpose_r(r, c):
            r_banks_of[r, c] = []
            for half in range(PACK // 2):
                r_bank = psum_r.tile([P, 2, TOK], F32, name="r_bank")
                for i in range(2):
                    for j in range(TILES):
                        nc.tensor.transpose(
                            r_bank[:, i, j * P : (j + 1) * P],
                            r_of[r][:, j, 2 * half + i, c * P : (c + 1) * P],
                            ident[:],
                        )
                r_banks_of[r, c].append(r_bank)

        def transpose_s(r, c):
            for j in range(TILES):
                s_bank_of[r, c, j] = psum_s.tile([P, PACK, P], F32, name="s_bank")
                for t in range(PACK):
                    nc.tensor.transpose(
                        s_bank_of[r, c, j][:, t, :], s_of[r][:, j, t, c * P : (c + 1) * P], ident[:]
                    )

        def affine(r, c):
            rn_of[r, c] = t_pool.tile([P, PACK, TOK], F32, name="rn_t")
            for t in range(PACK):
                m = c * PACK + t
                nc.scalar.activation(
                    out=rn_of[r, c][:, t, :], in_=r_banks_of[r, c][t // 2][:, t % 2, :], func=ACT.Identity,
                    scale=weight_col[:, m : m + 1], bias=bias_col[:, m : m + 1],
                )

        def product(r, c, j):
            if c == 0 and j == 0:
                gate_of[r] = q_pool.tile([P, PASSES, TOK, PACK], BF16, name="gate", align_bytes=64)
            tokens = slice(j * P, (j + 1) * P)
            nc.vector.tensor_tensor(
                out=gate_of[r][:, c, tokens, :].rearrange("p (q i) t -> p q t i", i=PAIR),
                in0=rn_of[r, c][:, :, tokens].rearrange("p t (q i) -> p q t i", i=PAIR),
                in1=s_bank_of[r, c, j][:].rearrange("p t (q i) -> p q t i", i=PAIR),
                op=ALU.mult,
            )

        def quantise(r):
            codes_of[r] = q_pool.tile([P, PASSES, TOK], U32, name="codes", align_bytes=64)
            scales_of[r] = q_pool.tile([P, PASSES, TOK], U8, name="scales", align_bytes=64)
            nc.vector.quantize_mx(
                out=codes_of[r][:].rearrange("p c k -> p (c k)").bitcast(FP8X4),
                scales=scales_of[r][:].rearrange("p c k -> p (c k)"),
                in_=gate_of[r][:].rearrange("p c k t -> p (c k t)"),
            )

        def matmuls(r, j, n):
            tokens = slice(j * P, (j + 1) * P)
            n_cols = slice(n * N_BANK, (n + 1) * N_BANK)
            if j == 0 and n == 0:
                out_of[r] = o_pool.tile([P, TILES, E], F32, name="out_sb")
            acc_of[r, j, n] = psum_o.tile([P, N_BANK], F32, name="acc")
            for c in range(PASSES):
                nc.tensor.matmul_mx(
                    out=acc_of[r, j, n][:],
                    lhsT=codes_of[r][:, c, tokens].bitcast(FP8X4),
                    lhsT_scale=scales_of[r][:, c, tokens],
                    rhs=w_codes[:, c, n_cols].bitcast(FP8X4),
                    rhs_scale=w_scales[:, c, n_cols],
                    start=(c == 0),
                    stop=(c == PASSES - 1),
                )

        def add_bias(r, j, n):
            n_cols = slice(n * N_BANK, (n + 1) * N_BANK)
            nc.vector.tensor_tensor(
                out=out_of[r][:, j, n_cols], in0=b_all[:, n_cols], in1=acc_of[r, j, n][:], op=ALU.add
            )

        def empty_bank(r, j, n):
            n_cols = slice(n * N_BANK, (n + 1) * N_BANK)
            nc.scalar.activation(out=out_of[r][:, j, n_cols], in_=acc_of[r, j, n][:], func=ACT.Identity)

        def add_bias_in_sbuf(r, j, n):
            n_cols = slice(n * N_BANK, (n + 1) * N_BANK)
            nc.gpsimd.tensor_tensor(
                out=out_of[r][:, j, n_cols], in0=out_of[r][:, j, n_cols], in1=b_all[:, n_cols], op=ALU.add
            )

        def store(r):
            nc.sync.dma_start(out=out_rounds[r], in_=out_of[r][:])

        def store_quarter(r, j, n):
            n_cols = slice(n * N_BANK, (n + 1) * N_BANK)
            nc.sync.dma_start(out=out_rounds[r][:, j, n_cols], in_=out_of[r][:, j, n_cols])

        def load_w(c):
            w_raw_of[c] = w_stage.tile([P, PACK, E], BF16, name="w_raw")
            nc.sync.dma_start(out=w_raw_of[c][:], in_=w_passes[c])

        def regroup_w(c):
            w_grouped_of[c] = w_stage.tile([P, E, PACK], BF16, name="w_grouped", align_bytes=64)
            nc.vector.tensor_copy(
                out=w_grouped_of[c][:].rearrange("p (q i) t -> p q t i", i=RUN),
                in_=w_raw_of[c][:].rearrange("p t (q i) -> p q t i", i=RUN),
            )

        def quantise_w(c):
            nc.vector.quantize_mx(
                out=w_codes[:, c, :].bitcast(FP8X4),
                scales=w_scales[:, c, :],
                in_=w_grouped_of[c][:].rearrange("p n t -> p (n t)"),
            )

        ident = const.tile([P, P], F32, name="ident")
        make_identity(nc, ident[:])
        minus_half = const.tile([P, GROUPS], F32, name="minus_half")
        nc.gpsimd.memset(minus_half[:], -0.5)
        w_codes = const.tile([P, PASSES, E], U32, name="w_codes", align_bytes=64)
        w_scales = const.tile([P, PASSES, E], U8, name="w_scales", align_bytes=64)

        weight_raw = const.tile([P, PASSES, PACK], BF16, name="weight_raw")
        bias_raw = const.tile([P, PASSES, PACK], BF16, name="bias_raw")
        weight_col = const.tile([P, PASSES * PACK], F32, name="weight_col")
        bias_col = const.tile([P, PASSES * PACK], F32, name="bias_col")

        b_all = const.tile([P, E], BF16, name="b_all")

        def pool_quarters(r):
            return QUARTERS[:1] if r < ROUNDS - 1 else []

        def live(r):
            return 0 <= r < ROUNDS

        first_step = -6
        for step in range(first_step, ROUNDS + 2):
            if live(step + AHEAD + 2):
                load_ret(step + AHEAD + 2)
            if live(step + 5):
                load_g(step + 5)
            if step == first_step + 1:
                nc.sync.dma_start(out=weight_raw[:], in_=gn_weight.rearrange("(c p t) -> p c t", t=PACK, p=P))
                nc.sync.dma_start(out=bias_raw[:], in_=gn_bias.rearrange("(c p t) -> p c t", t=PACK, p=P))
            if 0 <= step - (first_step + 2) < PASSES:
                load_w(step - (first_step + 2))
            if step == first_step + 4:
                nc.sync.dma_start(out=b_all[:], in_=b_o.partition_broadcast(P))

            if live(step + 3):
                inverse_deviation(step + 3)

            for j in range(TILES):
                for n in range(N_HALVES):
                    if n == 0 and live(step + 1):
                        transpose_r(step + 1, j)
                        affine(step + 1, j)
                    s_round, s_pass = (step, 1) if j == 0 else (step + 1, 0)
                    if n == 1 and live(s_round):
                        transpose_s(s_round, s_pass)
                    if live(step - 1):
                        matmuls(step - 1, j, n)
                    if live(step - 1) and (j, n) in pool_quarters(step - 1):
                        empty_bank(step - 1, j, n)
                    if live(step):
                        product(step, j, n)
                    b_round = step - 1 if (j, n) != QUARTERS[0] else step - 2
                    b_quarter = QUARTERS[QUARTERS.index((j, n)) - 1]
                    if live(b_round):
                        if b_quarter in pool_quarters(b_round):
                            add_bias_in_sbuf(b_round, *b_quarter)
                        else:
                            add_bias(b_round, *b_quarter)
                        if b_round == ROUNDS - 1:
                            store_quarter(b_round, *b_quarter)
                        elif b_quarter == QUARTERS[-1]:
                            store(b_round)
                    if live(step) and (j, n) == (TILES - 1, N_HALVES - 1):
                        quantise(step)
                    if live(step + AHEAD):
                        statistics(step + AHEAD, j, n)
                if j == 0 and live(step + 2):
                    normalise(step + 2, 0)
                    normalise(step + 2, 1)
                if j == 1 and live(step + 3):
                    swish(step + 3)
            if step == -3:
                nc.vector.tensor_copy(out=weight_col[:], in_=weight_raw[:].rearrange("p c t -> p (c t)"))
                nc.vector.tensor_copy(out=bias_col[:], in_=bias_raw[:].rearrange("p c t -> p (c t)"))
            if 0 <= step - (-1) < PASSES:
                quantise_w(step - (-1))
            if 0 <= step - (-2) < PASSES:
                regroup_w(step - (-2))
